import numpy as np
import ml_dtypes


def mxq(x, axis, fmt="e4m3"):
    dtype, down = {"e4m3": (ml_dtypes.float8_e4m3fn, 7), "e5m2": (ml_dtypes.float8_e5m2, 14)}[fmt]
    v = np.moveaxis(np.asarray(x, np.float32).astype(ml_dtypes.bfloat16).astype(np.float64), axis, -1)
    blocks = v.reshape(v.shape[:-1] + (-1, 32))
    amax = np.abs(blocks).max(-1, keepdims=True)
    byte = np.maximum(np.where(amax > 0, np.frexp(amax)[1] - 1 + 127, 0) - down, 1)
    scale = np.exp2(byte - 127.0)
    codes = (blocks / scale).astype(np.float32).astype(dtype).astype(np.float64)
    return np.moveaxis((codes * scale).reshape(v.shape), -1, axis)


WIDE = False


def mx_kscale(k):
    if not WIDE:
        return np.ones(k)
    levels = np.array([10, -10, 5, -5, 0])
    a = np.random.permutation(np.resize(levels, k // 512 * 4)).reshape(k // 512, 4)
    idx = np.arange(k)
    return np.exp2(a[idx // 512, idx % 128 // 32])


BF16 = ml_dtypes.bfloat16


def bf(x):
    return np.asarray(x, np.float32).astype(BF16)


def f64(x):
    return np.asarray(x).astype(np.float64)


E2M1 = np.array([0.0, 0.5, 1.0, 1.5, 2.0, 3.0, 4.0, 6.0, -0.0, -0.5, -1.0, -1.5, -2.0, -3.0, -4.0, -6.0])


def pack_weight(w, fmt):
    k, n = w.shape
    w = f64(bf(w)).reshape(k // 32, 32, n)
    amax = np.abs(w).max(1)
    if fmt == "e4m3":
        byte = np.frexp(amax)[1] - 1 + 127 - 7
    else:
        mant, ex = np.frexp(amax / 6.0)
        byte = np.where(mant > 0.5, ex, ex - 1) + 127
    byte = np.clip(np.where(amax > 0, byte, 1), 1, 254)
    scaled = (w * np.exp2(127.0 - byte)[:, None, :]).reshape(k, n).astype(np.float32)
    by_word = np.ascontiguousarray(scaled.reshape(k // 512, 128, 4, n).transpose(0, 1, 3, 2))
    if fmt == "e4m3":
        words = by_word.astype(ml_dtypes.float8_e4m3fn).view(np.uint8)
    else:
        c = by_word.astype(ml_dtypes.float4_e2m1fn).view(np.uint8) & 0xF
        words = c[..., 0::2] | (c[..., 1::2] << 4)
    return np.ascontiguousarray(words), np.ascontiguousarray(byte.astype(np.uint8).reshape(k // 512, 16, n))


def unpack_weight(words, scales, fmt):
    g, p, n, _ = words.shape
    if fmt == "e4m3":
        vals = np.ascontiguousarray(words).view(ml_dtypes.float8_e4m3fn).astype(np.float64)
    else:
        nib = np.empty((g, p, n, 4), np.uint8)
        nib[..., 0::2] = words & 0xF
        nib[..., 1::2] = words >> 4
        vals = E2M1[nib]
    vals = vals * np.repeat(np.exp2(scales.astype(np.float64) - 127.0), 8, axis=1)[..., None]
    return vals.transpose(0, 1, 3, 2).reshape(g * 512, n)


B, A, E, P, R = 1024, 8, 512, 512, 1024


def setup_inputs():
    s = mx_kscale(R)
    attr_rep = bf(np.random.standard_normal((B, A, R)) * s)
    stack = np.random.standard_normal((A, R, P)) / np.sqrt(R) / s[:, None]
    words, scales = pack_weight(stack.reshape(-1, P), "e4m3")
    self_weighted = bf(1.0 + 0.3 * np.random.standard_normal((1, A, 1)))
    return {
        "attr_rep": attr_rep,
        "bwd_proj_words": words,
        "bwd_proj_scales": scales,
        "self_weighted": self_weighted,
    }


def reference(attr_rep, bwd_proj_words, bwd_proj_scales, self_weighted):
    proj = (mxq(f64(attr_rep).transpose(1, 0, 2), 2, "e4m3") @ unpack_weight(bwd_proj_words, bwd_proj_scales, "e4m3").reshape(A, R, P)).transpose(1, 0, 2)
    return np.sum(np.maximum(proj, 0.0) * f64(self_weighted), axis=1)

@@ -1,0 +1,182 @@
+from contextlib import ExitStack
+
+import concourse.mybir as mybir
+from concourse.masks import make_identity
+
+BF16 = mybir.dt.bfloat16
+F32 = mybir.dt.float32
+I32 = mybir.dt.int32
+U32 = mybir.dt.uint32
+U8 = mybir.dt.uint8
+FP8X4 = mybir.dt.float8_e4m3fn_x4
+ALU = mybir.AluOpType
+RELU = mybir.ActivationFunctionType.Relu
+
+P = 128
+PACK = 4
+K_PASS = P * PACK
+
+NODES, TYPES, K, N = 1024, 8, 1024, 512
+NODE_TILES = NODES // P
+PASSES = K // K_PASS
+HALVES = 2
+PLANES_PER_TILE = 4
+PLANE_SETS = TYPES * PASSES // PLANES_PER_TILE
+QUADRANTS = 4
+
+UNITS_PER_RUN = 4
+RUNS_PER_TYPE = NODE_TILES // UNITS_PER_RUN
+RUNS = TYPES * RUNS_PER_TYPE
+
+FLOPS = 2 * NODES * TYPES * K * N
+
+
+def tile_attributegnn_pb_t_e_kernel(
+    tc, attr_rep, bwd_proj_words, bwd_proj_scales, self_weighted, out
+):
+    nc = tc.nc
+    words_dram = bwd_proj_words.rearrange("g p n t -> g p (n t)").bitcast(I32)
+    scales_dram = bwd_proj_scales.bitcast(I32)
+
+    with ExitStack() as stack:
+        const = stack.enter_context(tc.tile_pool(name="const", bufs=1))
+        x_pool = stack.enter_context(tc.tile_pool(name="x", bufs=TYPES * NODE_TILES))
+        w_pool = stack.enter_context(tc.tile_pool(name="w", bufs=TYPES))
+        acc_pool = stack.enter_context(tc.tile_pool(name="acc", bufs=NODE_TILES))
+        quant_pool = stack.enter_context(tc.tile_pool(name="quant", bufs=2))
+        relu_pool = stack.enter_context(tc.tile_pool(name="relu", bufs=UNITS_PER_RUN))
+        xt_pool = stack.enter_context(tc.psum_pool(name="xt", bufs=UNITS_PER_RUN))
+        proj_pool = stack.enter_context(tc.psum_pool(name="proj", bufs=UNITS_PER_RUN))
+        stack.enter_context(tc.manual_schedule())
+
+        type_weight_bf16 = const.tile([P, TYPES], BF16)
+        nc.scalar.dma_start(
+            out=type_weight_bf16[:],
+            in_=self_weighted.rearrange("o a i -> (o a i)").partition_broadcast(P),
+        )
+        w_planes = const.tile([P, PLANE_SETS, N], U8, align_bytes=64)
+        nc.vector.memset(w_planes[:].bitcast(I32), 0)
+        type_weight = const.tile([P, TYPES], F32)
+        nc.vector.tensor_copy(out=type_weight[:], in_=type_weight_bf16[:])
+        identity = const.tile([P, P], F32)
+        make_identity(nc, identity[:])
+
+        x_units = {}
+        w_words = {}
+        for a in range(TYPES):
+            for bt in range(NODE_TILES):
+                x_unit = x_pool.tile([P, K], BF16)
+                nc.sync.dma_start(out=x_unit[:], in_=attr_rep[P * bt : P * (bt + 1), a, :])
+                x_units[(a, bt)] = x_unit
+            if a % 2 == 0:
+                plane_set = a // 2
+                for quadrant in range(QUADRANTS):
+                    nc.sync.dma_start(
+                        out=w_planes[
+                            32 * quadrant : 32 * quadrant + 4 * PLANES_PER_TILE, plane_set, :
+                        ].bitcast(I32),
+                        in_=scales_dram[
+                            PLANES_PER_TILE * plane_set : PLANES_PER_TILE * (plane_set + 1),
+                            4 * quadrant : 4 * quadrant + 4,
+                            :,
+                        ],
+                    )
+            w_a = w_pool.tile([P, PASSES, PACK * N], U8, align_bytes=64)
+            nc.sync.dma_start(
+                out=w_a[:].bitcast(I32),
+                in_=words_dram[PASSES * a : PASSES * (a + 1)].rearrange("g p w -> p g w"),
+            )
+            w_words[a] = w_a
+
+        acc = []
+        for bt in range(NODE_TILES):
+            acc_bt = acc_pool.tile([P, N], F32)
+            acc.append(acc_bt)
+
+        def units_of(run):
+            a = run // RUNS_PER_TYPE
+            first_tile = UNITS_PER_RUN * (run % RUNS_PER_TYPE)
+            return [(a, first_tile + j) for j in range(UNITS_PER_RUN)]
+
+        def transpose_run(run):
+            grouped = quant_pool.tile([P, UNITS_PER_RUN, PASSES, P, PACK], BF16, align_bytes=64)
+            for j, unit in enumerate(units_of(run)):
+                x_f32 = x_units[unit][:].bitcast(F32)
+                xt = xt_pool.tile([P, PASSES, HALVES, P], F32)
+                for g in range(PASSES):
+                    for u in range(HALVES):
+                        nc.tensor.transpose(
+                            xt[:, g, u, :],
+                            x_f32[:, g * K_PASS // 2 + u : (g + 1) * K_PASS // 2 : HALVES],
+                            identity[:],
+                        )
+                copy_out = nc.vector.tensor_copy if j == UNITS_PER_RUN - 1 else nc.scalar.copy
+                copy_out(
+                    out=grouped[:, j].bitcast(F32),
+                    in_=xt[:].rearrange("p g u b -> p g b u"),
+                )
+            return grouped
+
+        def quantise_run(grouped):
+            codes = quant_pool.tile([P, UNITS_PER_RUN, PASSES, P], U32, align_bytes=64)
+            planes = quant_pool.tile([P, UNITS_PER_RUN, PASSES, P], U8, align_bytes=64)
+            nc.vector.quantize_mx(
+                out=codes[:].rearrange("p j g b -> p (j g b)").bitcast(FP8X4),
+                scales=planes[:].rearrange("p j g b -> p (j g b)"),
+                in_=grouped[:].rearrange("p j g b t -> p (j g b t)"),
+            )
+            return codes, planes
+
+        def multiply_run(run, codes, planes):
+            products = []
+            for j, (a, bt) in enumerate(units_of(run)):
+                proj = proj_pool.tile([P, N], F32)
+                for g in range(PASSES):
+                    plane_index = (PASSES * a + g) % PLANES_PER_TILE
+                    nc.tensor.matmul_mx(
+                        out=proj[:],
+                        lhsT=codes[:, j, g, :].bitcast(FP8X4),
+                        lhsT_scale=planes[:, j, g, :],
+                        rhs=w_words[a][:, g, :].bitcast(FP8X4),
+                        rhs_scale=w_planes[4 * plane_index : P, (PASSES * a + g) // PLANES_PER_TILE, :],
+                        start=(g == 0),
+                        stop=(g == PASSES - 1),
+                    )
+                products.append(proj)
+            return products
+
+        def add_run(run, products):
+            for (a, bt), proj in zip(units_of(run), products):
+                if a == 0:
+                    nc.vector.tensor_scalar(
+                        out=acc[bt][:],
+                        in0=proj[:],
+                        scalar1=0.0,
+                        scalar2=type_weight[:, 0:1],
+                        op0=ALU.max,
+                        op1=ALU.mult,
+                    )
+                else:
+                    relu = relu_pool.tile([P, N], F32)
+                    nc.scalar.activation(out=relu[:], in_=proj[:], func=RELU)
+                    nc.vector.scalar_tensor_tensor(
+                        out=acc[bt][:],
+                        in0=relu[:],
+                        scalar=type_weight[:, a : a + 1],
+                        in1=acc[bt][:],
+                        op0=ALU.mult,
+                        op1=ALU.add,
+                    )
+                if a == TYPES - 1:
+                    nc.sync.dma_start(out=out[P * bt : P * (bt + 1), :], in_=acc[bt][:])
+
+        quantised = None
+        for run in range(RUNS + 1):
+            if run < RUNS:
+                grouped = transpose_run(run)
+            if run > 0:
+                products = multiply_run(run - 1, quantised[0], quantised[1])
+            if run < RUNS:
+                quantised = quantise_run(grouped)
+            if run > 0:
+                add_run(run - 1, products)

@@ -28,6 +28,9 @@ UNITS_PER_RUN = 4
 RUNS_PER_TYPE = NODE_TILES // UNITS_PER_RUN
 RUNS = TYPES * RUNS_PER_TYPE
 
+SORTED_PLACES = (1, 3)
+FIRST_SORTED_RUN = 2
+
 FLOPS = 2 * NODES * TYPES * K * N
 
 
@@ -45,6 +48,7 @@ def tile_attributegnn_pb_t_e_kernel(
         acc_pool = stack.enter_context(tc.tile_pool(name="acc", bufs=NODE_TILES))
         quant_pool = stack.enter_context(tc.tile_pool(name="quant", bufs=2))
         relu_pool = stack.enter_context(tc.tile_pool(name="relu", bufs=UNITS_PER_RUN))
+        sort_pool = stack.enter_context(tc.tile_pool(name="sort", bufs=2 * len(SORTED_PLACES)))
         xt_pool = stack.enter_context(tc.psum_pool(name="xt", bufs=UNITS_PER_RUN))
         proj_pool = stack.enter_context(tc.psum_pool(name="proj", bufs=UNITS_PER_RUN))
         stack.enter_context(tc.manual_schedule())
@@ -98,19 +102,40 @@ def tile_attributegnn_pb_t_e_kernel(
             first_tile = UNITS_PER_RUN * (run % RUNS_PER_TYPE)
             return [(a, first_tile + j) for j in range(UNITS_PER_RUN)]
 
+        sorted_units = {}
+
+        def sort_run(run):
+            if run < FIRST_SORTED_RUN or run >= RUNS:
+                return
+            for j, unit in enumerate(units_of(run)):
+                if j in SORTED_PLACES:
+                    sorted_words = sort_pool.tile([P, K], BF16)
+                    nc.vector.tensor_copy(
+                        out=sorted_words[:]
+                        .bitcast(F32)
+                        .rearrange("b (g u p) -> b g u p", g=PASSES, u=HALVES),
+                        in_=x_units[unit][:]
+                        .bitcast(F32)
+                        .rearrange("b (g p u) -> b g u p", g=PASSES, u=HALVES),
+                    )
+                    sorted_units[unit] = sorted_words
+
         def transpose_run(run):
             grouped = quant_pool.tile([P, UNITS_PER_RUN, PASSES, P, PACK], BF16, align_bytes=64)
             for j, unit in enumerate(units_of(run)):
-                x_f32 = x_units[unit][:].bitcast(F32)
                 xt = xt_pool.tile([P, PASSES, HALVES, P], F32)
                 for g in range(PASSES):
                     for u in range(HALVES):
-                        nc.tensor.transpose(
-                            xt[:, g, u, :],
-                            x_f32[:, g * K_PASS // 2 + u : (g + 1) * K_PASS // 2 : HALVES],
-                            identity[:],
-                        )
-                copy_out = nc.vector.tensor_copy if j == UNITS_PER_RUN - 1 else nc.scalar.copy
+                        if unit in sorted_units:
+                            first = (g * HALVES + u) * P
+                            words = sorted_units[unit][:].bitcast(F32)[:, first : first + P]
+                        else:
+                            words = x_units[unit][:].bitcast(F32)[
+                                :, g * K_PASS // 2 + u : (g + 1) * K_PASS // 2 : HALVES
+                            ]
+                        nc.tensor.transpose(xt[:, g, u, :], words, identity[:])
+                on_vector = j == UNITS_PER_RUN - 1 and run % 2 == 0
+                copy_out = nc.vector.tensor_copy if on_vector else nc.scalar.copy
                 copy_out(
                     out=grouped[:, j].bitcast(F32),
                     in_=xt[:].rearrange("p g u b -> p g b u"),
@@ -178,5 +203,6 @@ def tile_attributegnn_pb_t_e_kernel(
                 products = multiply_run(run - 1, quantised[0], quantised[1])
             if run < RUNS:
                 quantised = quantise_run(grouped)
+            sort_run(run + 1)
             if run > 0:
                 add_run(run - 1, products)

@@ -29,7 +29,7 @@ RUNS_PER_TYPE = NODE_TILES // UNITS_PER_RUN
 RUNS = TYPES * RUNS_PER_TYPE
 
 SORTED_PLACES = (1, 3)
-FIRST_SORTED_RUN = 2
+FIRST_SORTED_RUN = 3
 
 FLOPS = 2 * NODES * TYPES * K * N
 
@@ -197,12 +197,12 @@ def tile_attributegnn_pb_t_e_kernel(
 
         quantised = None
         for run in range(RUNS + 1):
+            sort_run(run + 1)
             if run < RUNS:
                 grouped = transpose_run(run)
             if run > 0:
                 products = multiply_run(run - 1, quantised[0], quantised[1])
             if run < RUNS:
                 quantised = quantise_run(grouped)
-            sort_run(run + 1)
             if run > 0:
                 add_run(run - 1, products)

@@ -105,7 +105,7 @@ def tile_attributegnn_pb_t_e_kernel(
         sorted_units = {}
 
         def sort_run(run):
-            if run < FIRST_SORTED_RUN or run >= RUNS:
+            if run < FIRST_SORTED_RUN or run >= RUNS or run % 2 == 1:
                 return
             for j, unit in enumerate(units_of(run)):
                 if j in SORTED_PLACES:

@@ -10,7 +10,8 @@ U32 = mybir.dt.uint32
 U8 = mybir.dt.uint8
 FP8X4 = mybir.dt.float8_e4m3fn_x4
 ALU = mybir.AluOpType
-RELU = mybir.ActivationFunctionType.Relu
+AXIS = mybir.AxisListType
+COPY = mybir.ActivationFunctionType.Copy
 
 P = 128
 PACK = 4
@@ -28,8 +29,11 @@ UNITS_PER_RUN = 4
 RUNS_PER_TYPE = NODE_TILES // UNITS_PER_RUN
 RUNS = TYPES * RUNS_PER_TYPE
 
-SORTED_PLACES = (1, 3)
-FIRST_SORTED_RUN = 3
+SORTED_PLACES = (1, 2, 3)
+FIRST_SORTED_RUN = 2
+
+SMALLEST_PART = 2.0 ** -40
+SMALLEST_WEIGHT = 1e-30
 
 FLOPS = 2 * NODES * TYPES * K * N
 
@@ -45,9 +49,8 @@ def tile_attributegnn_pb_t_e_kernel(
         const = stack.enter_context(tc.tile_pool(name="const", bufs=1))
         x_pool = stack.enter_context(tc.tile_pool(name="x", bufs=TYPES * NODE_TILES))
         w_pool = stack.enter_context(tc.tile_pool(name="w", bufs=TYPES))
-        acc_pool = stack.enter_context(tc.tile_pool(name="acc", bufs=NODE_TILES))
         quant_pool = stack.enter_context(tc.tile_pool(name="quant", bufs=2))
-        relu_pool = stack.enter_context(tc.tile_pool(name="relu", bufs=UNITS_PER_RUN))
+        gate_pool = stack.enter_context(tc.tile_pool(name="gate", bufs=2))
         sort_pool = stack.enter_context(tc.tile_pool(name="sort", bufs=2 * len(SORTED_PLACES)))
         xt_pool = stack.enter_context(tc.psum_pool(name="xt", bufs=UNITS_PER_RUN))
         proj_pool = stack.enter_context(tc.psum_pool(name="proj", bufs=UNITS_PER_RUN))
@@ -64,6 +67,51 @@ def tile_attributegnn_pb_t_e_kernel(
         nc.vector.tensor_copy(out=type_weight[:], in_=type_weight_bf16[:])
         identity = const.tile([P, P], F32)
         make_identity(nc, identity[:])
+
+        negated = const.tile([P, TYPES], F32)
+        nc.vector.tensor_scalar(
+            out=negated[:], in0=type_weight[:], scalar1=-1.0, scalar2=None, op0=ALU.mult
+        )
+        magnitude = const.tile([P, TYPES], F32)
+        nc.vector.tensor_tensor(out=magnitude[:], in0=type_weight[:], in1=negated[:], op=ALU.max)
+        floor = const.tile([P, 1], F32)
+        nc.vector.tensor_reduce(out=floor[:], in_=magnitude[:], axis=AXIS.X, op=ALU.max)
+        nc.vector.tensor_scalar(
+            out=floor[:],
+            in0=floor[:],
+            scalar1=SMALLEST_PART,
+            scalar2=SMALLEST_WEIGHT,
+            op0=ALU.mult,
+            op1=ALU.add,
+        )
+        large = const.tile([P, TYPES], F32)
+        nc.vector.tensor_scalar(
+            out=large[:], in0=magnitude[:], scalar1=floor[:, 0:1], scalar2=None, op0=ALU.is_ge
+        )
+        kept = const.tile([P, TYPES], F32)
+        nc.vector.tensor_tensor(out=kept[:], in0=type_weight[:], in1=large[:], op=ALU.mult)
+        small = const.tile([P, TYPES], F32)
+        nc.vector.tensor_scalar(
+            out=small[:], in0=large[:], scalar1=-1.0, scalar2=1.0, op0=ALU.mult, op1=ALU.add
+        )
+        divisor = const.tile([P, TYPES], F32)
+        nc.vector.scalar_tensor_tensor(
+            out=divisor[:],
+            in0=small[:],
+            scalar=floor[:, 0:1],
+            in1=kept[:],
+            op0=ALU.mult,
+            op1=ALU.add,
+        )
+        inverse = const.tile([P, TYPES], F32)
+        nc.vector.reciprocal(out=inverse[:], in_=divisor[:])
+        step = const.tile([P, TYPES], F32)
+        nc.vector.tensor_tensor(
+            out=step[:, 0 : TYPES - 1],
+            in0=divisor[:, 0 : TYPES - 1],
+            in1=inverse[:, 1:TYPES],
+            op=ALU.mult,
+        )
 
         x_units = {}
         w_words = {}
@@ -92,10 +140,7 @@ def tile_attributegnn_pb_t_e_kernel(
             )
             w_words[a] = w_a
 
-        acc = []
-        for bt in range(NODE_TILES):
-            acc_bt = acc_pool.tile([P, N], F32)
-            acc.append(acc_bt)
+        acc = const.tile([P, NODE_TILES, N], F32)
 
         def units_of(run):
             a = run // RUNS_PER_TYPE
@@ -105,12 +150,12 @@ def tile_attributegnn_pb_t_e_kernel(
         sorted_units = {}
 
         def sort_run(run):
-            if run < FIRST_SORTED_RUN or run >= RUNS or run % 2 == 1:
+            if run < FIRST_SORTED_RUN or run >= RUNS:
                 return
             for j, unit in enumerate(units_of(run)):
                 if j in SORTED_PLACES:
                     sorted_words = sort_pool.tile([P, K], BF16)
-                    nc.vector.tensor_copy(
+                    nc.scalar.copy(
                         out=sorted_words[:]
                         .bitcast(F32)
                         .rearrange("b (g u p) -> b g u p", g=PASSES, u=HALVES),
@@ -134,9 +179,7 @@ def tile_attributegnn_pb_t_e_kernel(
                                 :, g * K_PASS // 2 + u : (g + 1) * K_PASS // 2 : HALVES
                             ]
                         nc.tensor.transpose(xt[:, g, u, :], words, identity[:])
-                on_vector = j == UNITS_PER_RUN - 1 and run % 2 == 0
-                copy_out = nc.vector.tensor_copy if on_vector else nc.scalar.copy
-                copy_out(
+                nc.scalar.copy(
                     out=grouped[:, j].bitcast(F32),
                     in_=xt[:].rearrange("p g u b -> p g b u"),
                 )
@@ -170,39 +213,67 @@ def tile_attributegnn_pb_t_e_kernel(
                 products.append(proj)
             return products
 
-        def add_run(run, products):
-            for (a, bt), proj in zip(units_of(run), products):
+        def add_units(run, products, places):
+            for j in places:
+                a, bt = units_of(run)[j]
+                proj = products[j]
                 if a == 0:
                     nc.vector.tensor_scalar(
-                        out=acc[bt][:],
-                        in0=proj[:],
-                        scalar1=0.0,
-                        scalar2=type_weight[:, 0:1],
-                        op0=ALU.max,
-                        op1=ALU.mult,
+                        out=acc[:, bt, :], in0=proj[:], scalar1=0.0, scalar2=None, op0=ALU.max
                     )
                 else:
-                    relu = relu_pool.tile([P, N], F32)
-                    nc.scalar.activation(out=relu[:], in_=proj[:], func=RELU)
                     nc.vector.scalar_tensor_tensor(
-                        out=acc[bt][:],
-                        in0=relu[:],
-                        scalar=type_weight[:, a : a + 1],
-                        in1=acc[bt][:],
-                        op0=ALU.mult,
+                        out=acc[:, bt, :],
+                        in0=proj[:],
+                        scalar=0.0,
+                        in1=acc[:, bt, :],
+                        op0=ALU.max,
                         op1=ALU.add,
                     )
                 if a == TYPES - 1:
-                    nc.sync.dma_start(out=out[P * bt : P * (bt + 1), :], in_=acc[bt][:])
+                    nc.scalar.activation(
+                        out=acc[:, bt, :],
+                        in_=acc[:, bt, :],
+                        func=COPY,
+                        scale=divisor[:, a : a + 1],
+                    )
+                    nc.sync.dma_start(out=out[P * bt : P * (bt + 1), :], in_=acc[:, bt, :])
+
+        def rescale_run(run):
+            if run < 0:
+                return
+            a, first_tile = units_of(run)[0]
+            if a == TYPES - 1:
+                return
+            nc.vector.tensor_scalar(
+                out=acc[:, first_tile, :],
+                in0=acc[:, first_tile, :],
+                scalar1=step[:, a : a + 1],
+                scalar2=None,
+                op0=ALU.mult,
+            )
+            step_now = gate_pool.tile([P, 1], F32)
+            nc.vector.tensor_copy(out=step_now[:], in_=step[:, a : a + 1])
+            nc.gpsimd.tensor_scalar(
+                out=acc[:, first_tile + 1 : first_tile + UNITS_PER_RUN, :],
+                in0=acc[:, first_tile + 1 : first_tile + UNITS_PER_RUN, :],
+                scalar1=step_now[:, 0:1],
+                scalar2=0.0,
+                op0=ALU.mult,
+                op1=ALU.add,
+            )
 
         quantised = None
         for run in range(RUNS + 1):
-            sort_run(run + 1)
             if run < RUNS:
                 grouped = transpose_run(run)
             if run > 0:
                 products = multiply_run(run - 1, quantised[0], quantised[1])
+            sort_run(run + 1)
+            if run > 0:
+                add_units(run - 1, products, (0,))
             if run < RUNS:
                 quantised = quantise_run(grouped)
+            rescale_run(run - 2)
             if run > 0:
-                add_run(run - 1, products)
+                add_units(run - 1, products, (1, 2, 3))

@@ -29,7 +29,7 @@ UNITS_PER_RUN = 4
 RUNS_PER_TYPE = NODE_TILES // UNITS_PER_RUN
 RUNS = TYPES * RUNS_PER_TYPE
 
-SORTED_PLACES = (1, 2, 3)
+SORTED_PLACES = ((1, 2, 3), (2, 3))
 FIRST_SORTED_RUN = 2
 
 SMALLEST_PART = 2.0 ** -40
@@ -51,7 +51,7 @@ def tile_attributegnn_pb_t_e_kernel(
         w_pool = stack.enter_context(tc.tile_pool(name="w", bufs=TYPES))
         quant_pool = stack.enter_context(tc.tile_pool(name="quant", bufs=2))
         gate_pool = stack.enter_context(tc.tile_pool(name="gate", bufs=2))
-        sort_pool = stack.enter_context(tc.tile_pool(name="sort", bufs=2 * len(SORTED_PLACES)))
+        sort_pool = stack.enter_context(tc.tile_pool(name="sort", bufs=2 * len(SORTED_PLACES[0])))
         xt_pool = stack.enter_context(tc.psum_pool(name="xt", bufs=UNITS_PER_RUN))
         proj_pool = stack.enter_context(tc.psum_pool(name="proj", bufs=UNITS_PER_RUN))
         stack.enter_context(tc.manual_schedule())
@@ -153,7 +153,7 @@ def tile_attributegnn_pb_t_e_kernel(
             if run < FIRST_SORTED_RUN or run >= RUNS:
                 return
             for j, unit in enumerate(units_of(run)):
-                if j in SORTED_PLACES:
+                if j in SORTED_PLACES[run % 2]:
                     sorted_words = sort_pool.tile([P, K], BF16)
                     nc.scalar.copy(
                         out=sorted_words[:]
@@ -252,11 +252,15 @@ def tile_attributegnn_pb_t_e_kernel(
                 scalar2=None,
                 op0=ALU.mult,
             )
+            others = acc[:, first_tile + 1 : first_tile + UNITS_PER_RUN, :]
+            if run == RUNS - 3:
+                nc.scalar.activation(out=others, in_=others, func=COPY, scale=step[:, a : a + 1])
+                return
             step_now = gate_pool.tile([P, 1], F32)
             nc.vector.tensor_copy(out=step_now[:], in_=step[:, a : a + 1])
             nc.gpsimd.tensor_scalar(
-                out=acc[:, first_tile + 1 : first_tile + UNITS_PER_RUN, :],
-                in0=acc[:, first_tile + 1 : first_tile + UNITS_PER_RUN, :],
+                out=others,
+                in0=others,
                 scalar1=step_now[:, 0:1],
                 scalar2=0.0,
                 op0=ALU.mult,

@@ -29,7 +29,7 @@ UNITS_PER_RUN = 4
 RUNS_PER_TYPE = NODE_TILES // UNITS_PER_RUN
 RUNS = TYPES * RUNS_PER_TYPE
 
-SORTED_PLACES = ((1, 2, 3), (2, 3))
+SORTED_PLACES = ((2, 3), (2, 3))
 FIRST_SORTED_RUN = 2
 
 SMALLEST_PART = 2.0 ** -40
@@ -50,7 +50,7 @@ def tile_attributegnn_pb_t_e_kernel(
         x_pool = stack.enter_context(tc.tile_pool(name="x", bufs=TYPES * NODE_TILES))
         w_pool = stack.enter_context(tc.tile_pool(name="w", bufs=TYPES))
         quant_pool = stack.enter_context(tc.tile_pool(name="quant", bufs=2))
-        gate_pool = stack.enter_context(tc.tile_pool(name="gate", bufs=2))
+        gate_pool = stack.enter_context(tc.tile_pool(name="gate", bufs=1))
         sort_pool = stack.enter_context(tc.tile_pool(name="sort", bufs=2 * len(SORTED_PLACES[0])))
         xt_pool = stack.enter_context(tc.psum_pool(name="xt", bufs=UNITS_PER_RUN))
         proj_pool = stack.enter_context(tc.psum_pool(name="proj", bufs=UNITS_PER_RUN))
@@ -219,32 +219,38 @@ def tile_attributegnn_pb_t_e_kernel(
                 proj = products[j]
                 if a == 0:
                     nc.vector.tensor_scalar(
-                        out=acc[:, bt, :], in0=proj[:], scalar1=0.0, scalar2=None, op0=ALU.max
-                    )
-                else:
-                    nc.vector.scalar_tensor_tensor(
                         out=acc[:, bt, :],
                         in0=proj[:],
+                        scalar1=0.0,
+                        scalar2=step[:, 0:1],
+                        op0=ALU.max,
+                        op1=ALU.mult,
+                    )
+                    continue
+                last = a == TYPES - 1 and bt == NODE_TILES - 1
+                halves = ((0, N // 2), (N // 2, N)) if last else ((0, N),)
+                for first, end in halves:
+                    nc.vector.scalar_tensor_tensor(
+                        out=acc[:, bt, first:end],
+                        in0=proj[:, first:end],
                         scalar=0.0,
-                        in1=acc[:, bt, :],
+                        in1=acc[:, bt, first:end],
                         op0=ALU.max,
                         op1=ALU.add,
                     )
-                if a == TYPES - 1:
+                if a < TYPES - 1:
+                    continue
+                for first, end in halves:
+                    result = acc[:, bt, first:end]
                     nc.scalar.activation(
-                        out=acc[:, bt, :],
-                        in_=acc[:, bt, :],
-                        func=COPY,
-                        scale=divisor[:, a : a + 1],
+                        out=result, in_=result, func=COPY, scale=divisor[:, a : a + 1]
                     )
-                    nc.sync.dma_start(out=out[P * bt : P * (bt + 1), :], in_=acc[:, bt, :])
+                    nc.sync.dma_start(out=out[P * bt : P * (bt + 1), first:end], in_=result)
 
         def rescale_run(run):
-            if run < 0:
+            if run < RUNS_PER_TYPE or run >= RUNS - RUNS_PER_TYPE:
                 return
             a, first_tile = units_of(run)[0]
-            if a == TYPES - 1:
-                return
             nc.vector.tensor_scalar(
                 out=acc[:, first_tile, :],
                 in0=acc[:, first_tile, :],

from contextlib import ExitStack

import concourse.mybir as mybir
from concourse.masks import make_identity

BF16 = mybir.dt.bfloat16
F32 = mybir.dt.float32
I32 = mybir.dt.int32
U32 = mybir.dt.uint32
U8 = mybir.dt.uint8
FP8X4 = mybir.dt.float8_e4m3fn_x4
ALU = mybir.AluOpType
AXIS = mybir.AxisListType
COPY = mybir.ActivationFunctionType.Copy

P = 128
PACK = 4
K_PASS = P * PACK

NODES, TYPES, K, N = 1024, 8, 1024, 512
NODE_TILES = NODES // P
PASSES = K // K_PASS
HALVES = 2
PLANES_PER_TILE = 4
PLANE_SETS = TYPES * PASSES // PLANES_PER_TILE
QUADRANTS = 4

UNITS_PER_RUN = 4
RUNS_PER_TYPE = NODE_TILES // UNITS_PER_RUN
RUNS = TYPES * RUNS_PER_TYPE

SORTED_PLACES = ((2, 3), (2, 3))
FIRST_SORTED_RUN = 2

SMALLEST_PART = 2.0 ** -40
SMALLEST_WEIGHT = 1e-30

FLOPS = 2 * NODES * TYPES * K * N


def tile_attributegnn_pb_t_e_kernel(
    tc, attr_rep, bwd_proj_words, bwd_proj_scales, self_weighted, out
):
    nc = tc.nc
    words_dram = bwd_proj_words.rearrange("g p n t -> g p (n t)").bitcast(I32)
    scales_dram = bwd_proj_scales.bitcast(I32)

    with ExitStack() as stack:
        const = stack.enter_context(tc.tile_pool(name="const", bufs=1))
        x_pool = stack.enter_context(tc.tile_pool(name="x", bufs=TYPES * NODE_TILES))
        w_pool = stack.enter_context(tc.tile_pool(name="w", bufs=TYPES))
        quant_pool = stack.enter_context(tc.tile_pool(name="quant", bufs=2))
        gate_pool = stack.enter_context(tc.tile_pool(name="gate", bufs=1))
        sort_pool = stack.enter_context(tc.tile_pool(name="sort", bufs=2 * len(SORTED_PLACES[0])))
        xt_pool = stack.enter_context(tc.psum_pool(name="xt", bufs=UNITS_PER_RUN))
        proj_pool = stack.enter_context(tc.psum_pool(name="proj", bufs=UNITS_PER_RUN))
        stack.enter_context(tc.manual_schedule())

        type_weight_bf16 = const.tile([P, TYPES], BF16)
        nc.scalar.dma_start(
            out=type_weight_bf16[:],
            in_=self_weighted.rearrange("o a i -> (o a i)").partition_broadcast(P),
        )
        w_planes = const.tile([P, PLANE_SETS, N], U8, align_bytes=64)
        nc.vector.memset(w_planes[:].bitcast(I32), 0)
        type_weight = const.tile([P, TYPES], F32)
        nc.vector.tensor_copy(out=type_weight[:], in_=type_weight_bf16[:])
        identity = const.tile([P, P], F32)
        make_identity(nc, identity[:])

        negated = const.tile([P, TYPES], F32)
        nc.vector.tensor_scalar(
            out=negated[:], in0=type_weight[:], scalar1=-1.0, scalar2=None, op0=ALU.mult
        )
        magnitude = const.tile([P, TYPES], F32)
        nc.vector.tensor_tensor(out=magnitude[:], in0=type_weight[:], in1=negated[:], op=ALU.max)
        floor = const.tile([P, 1], F32)
        nc.vector.tensor_reduce(out=floor[:], in_=magnitude[:], axis=AXIS.X, op=ALU.max)
        nc.vector.tensor_scalar(
            out=floor[:],
            in0=floor[:],
            scalar1=SMALLEST_PART,
            scalar2=SMALLEST_WEIGHT,
            op0=ALU.mult,
            op1=ALU.add,
        )
        large = const.tile([P, TYPES], F32)
        nc.vector.tensor_scalar(
            out=large[:], in0=magnitude[:], scalar1=floor[:, 0:1], scalar2=None, op0=ALU.is_ge
        )
        kept = const.tile([P, TYPES], F32)
        nc.vector.tensor_tensor(out=kept[:], in0=type_weight[:], in1=large[:], op=ALU.mult)
        small = const.tile([P, TYPES], F32)
        nc.vector.tensor_scalar(
            out=small[:], in0=large[:], scalar1=-1.0, scalar2=1.0, op0=ALU.mult, op1=ALU.add
        )
        divisor = const.tile([P, TYPES], F32)
        nc.vector.scalar_tensor_tensor(
            out=divisor[:],
            in0=small[:],
            scalar=floor[:, 0:1],
            in1=kept[:],
            op0=ALU.mult,
            op1=ALU.add,
        )
        inverse = const.tile([P, TYPES], F32)
        nc.vector.reciprocal(out=inverse[:], in_=divisor[:])
        step = const.tile([P, TYPES], F32)
        nc.vector.tensor_tensor(
            out=step[:, 0 : TYPES - 1],
            in0=divisor[:, 0 : TYPES - 1],
            in1=inverse[:, 1:TYPES],
            op=ALU.mult,
        )

        x_units = {}
        w_words = {}
        for a in range(TYPES):
            for bt in range(NODE_TILES):
                x_unit = x_pool.tile([P, K], BF16)
                nc.sync.dma_start(out=x_unit[:], in_=attr_rep[P * bt : P * (bt + 1), a, :])
                x_units[(a, bt)] = x_unit
            if a % 2 == 0:
                plane_set = a // 2
                for quadrant in range(QUADRANTS):
                    nc.sync.dma_start(
                        out=w_planes[
                            32 * quadrant : 32 * quadrant + 4 * PLANES_PER_TILE, plane_set, :
                        ].bitcast(I32),
                        in_=scales_dram[
                            PLANES_PER_TILE * plane_set : PLANES_PER_TILE * (plane_set + 1),
                            4 * quadrant : 4 * quadrant + 4,
                            :,
                        ],
                    )
            w_a = w_pool.tile([P, PASSES, PACK * N], U8, align_bytes=64)
            nc.sync.dma_start(
                out=w_a[:].bitcast(I32),
                in_=words_dram[PASSES * a : PASSES * (a + 1)].rearrange("g p w -> p g w"),
            )
            w_words[a] = w_a

        acc = const.tile([P, NODE_TILES, N], F32)

        def units_of(run):
            a = run // RUNS_PER_TYPE
            first_tile = UNITS_PER_RUN * (run % RUNS_PER_TYPE)
            return [(a, first_tile + j) for j in range(UNITS_PER_RUN)]

        sorted_units = {}

        def sort_run(run):
            if run < FIRST_SORTED_RUN or run >= RUNS:
                return
            for j, unit in enumerate(units_of(run)):
                if j in SORTED_PLACES[run % 2]:
                    sorted_words = sort_pool.tile([P, K], BF16)
                    nc.scalar.copy(
                        out=sorted_words[:]
                        .bitcast(F32)
                        .rearrange("b (g u p) -> b g u p", g=PASSES, u=HALVES),
                        in_=x_units[unit][:]
                        .bitcast(F32)
                        .rearrange("b (g p u) -> b g u p", g=PASSES, u=HALVES),
                    )
                    sorted_units[unit] = sorted_words

        def transpose_run(run):
            grouped = quant_pool.tile([P, UNITS_PER_RUN, PASSES, P, PACK], BF16, align_bytes=64)
            for j, unit in enumerate(units_of(run)):
                xt = xt_pool.tile([P, PASSES, HALVES, P], F32)
                for g in range(PASSES):
                    for u in range(HALVES):
                        if unit in sorted_units:
                            first = (g * HALVES + u) * P
                            words = sorted_units[unit][:].bitcast(F32)[:, first : first + P]
                        else:
                            words = x_units[unit][:].bitcast(F32)[
                                :, g * K_PASS // 2 + u : (g + 1) * K_PASS // 2 : HALVES
                            ]
                        nc.tensor.transpose(xt[:, g, u, :], words, identity[:])
                nc.scalar.copy(
                    out=grouped[:, j].bitcast(F32),
                    in_=xt[:].rearrange("p g u b -> p g b u"),
                )
            return grouped

        def quantise_run(grouped):
            codes = quant_pool.tile([P, UNITS_PER_RUN, PASSES, P], U32, align_bytes=64)
            planes = quant_pool.tile([P, UNITS_PER_RUN, PASSES, P], U8, align_bytes=64)
            nc.vector.quantize_mx(
                out=codes[:].rearrange("p j g b -> p (j g b)").bitcast(FP8X4),
                scales=planes[:].rearrange("p j g b -> p (j g b)"),
                in_=grouped[:].rearrange("p j g b t -> p (j g b t)"),
            )
            return codes, planes

        def multiply_run(run, codes, planes):
            products = []
            for j, (a, bt) in enumerate(units_of(run)):
                proj = proj_pool.tile([P, N], F32)
                for g in range(PASSES):
                    plane_index = (PASSES * a + g) % PLANES_PER_TILE
                    nc.tensor.matmul_mx(
                        out=proj[:],
                        lhsT=codes[:, j, g, :].bitcast(FP8X4),
                        lhsT_scale=planes[:, j, g, :],
                        rhs=w_words[a][:, g, :].bitcast(FP8X4),
                        rhs_scale=w_planes[4 * plane_index : P, (PASSES * a + g) // PLANES_PER_TILE, :],
                        start=(g == 0),
                        stop=(g == PASSES - 1),
                    )
                products.append(proj)
            return products

        def add_units(run, products, places):
            for j in places:
                a, bt = units_of(run)[j]
                proj = products[j]
                if a == 0:
                    nc.vector.tensor_scalar(
                        out=acc[:, bt, :],
                        in0=proj[:],
                        scalar1=0.0,
                        scalar2=step[:, 0:1],
                        op0=ALU.max,
                        op1=ALU.mult,
                    )
                    continue
                last = a == TYPES - 1 and bt == NODE_TILES - 1
                halves = ((0, N // 2), (N // 2, N)) if last else ((0, N),)
                for first, end in halves:
                    nc.vector.scalar_tensor_tensor(
                        out=acc[:, bt, first:end],
                        in0=proj[:, first:end],
                        scalar=0.0,
                        in1=acc[:, bt, first:end],
                        op0=ALU.max,
                        op1=ALU.add,
                    )
                if a < TYPES - 1:
                    continue
                for first, end in halves:
                    result = acc[:, bt, first:end]
                    nc.scalar.activation(
                        out=result, in_=result, func=COPY, scale=divisor[:, a : a + 1]
                    )
                    nc.sync.dma_start(out=out[P * bt : P * (bt + 1), first:end], in_=result)

        def rescale_run(run):
            if run < RUNS_PER_TYPE or run >= RUNS - RUNS_PER_TYPE:
                return
            a, first_tile = units_of(run)[0]
            nc.vector.tensor_scalar(
                out=acc[:, first_tile, :],
                in0=acc[:, first_tile, :],
                scalar1=step[:, a : a + 1],
                scalar2=None,
                op0=ALU.mult,
            )
            others = acc[:, first_tile + 1 : first_tile + UNITS_PER_RUN, :]
            if run == RUNS - 3:
                nc.scalar.activation(out=others, in_=others, func=COPY, scale=step[:, a : a + 1])
                return
            step_now = gate_pool.tile([P, 1], F32)
            nc.vector.tensor_copy(out=step_now[:], in_=step[:, a : a + 1])
            nc.gpsimd.tensor_scalar(
                out=others,
                in0=others,
                scalar1=step_now[:, 0:1],
                scalar2=0.0,
                op0=ALU.mult,
                op1=ALU.add,
            )

        quantised = None
        for run in range(RUNS + 1):
            if run < RUNS:
                grouped = transpose_run(run)
            if run > 0:
                products = multiply_run(run - 1, quantised[0], quantised[1])
            sort_run(run + 1)
            if run > 0:
                add_units(run - 1, products, (0,))
            if run < RUNS:
                quantised = quantise_run(grouped)
            rescale_run(run - 2)
            if run > 0:
                add_units(run - 1, products, (1, 2, 3))
